import numpy as np
import ml_dtypes


def mxq(x, axis, fmt="e4m3"):
    dtype, down = {"e4m3": (ml_dtypes.float8_e4m3fn, 7), "e5m2": (ml_dtypes.float8_e5m2, 14)}[fmt]
    v = np.moveaxis(np.asarray(x, np.float32).astype(ml_dtypes.bfloat16).astype(np.float64), axis, -1)
    blocks = v.reshape(v.shape[:-1] + (-1, 32))
    amax = np.abs(blocks).max(-1, keepdims=True)
    byte = np.maximum(np.where(amax > 0, np.frexp(amax)[1] - 1 + 127, 0) - down, 1)
    scale = np.exp2(byte - 127.0)
    codes = (blocks / scale).astype(np.float32).astype(dtype).astype(np.float64)
    return np.moveaxis((codes * scale).reshape(v.shape), -1, axis)


WIDE = False


def mx_kscale(k):
    if not WIDE:
        return np.ones(k)
    levels = np.array([10, -10, 5, -5, 0])
    a = np.random.permutation(np.resize(levels, k // 512 * 4)).reshape(k // 512, 4)
    idx = np.arange(k)
    return np.exp2(a[idx // 512, idx % 128 // 32])


BF16 = ml_dtypes.bfloat16


def bf(x):
    return np.asarray(x, np.float32).astype(BF16)


def f64(x):
    return np.asarray(x).astype(np.float64)


E2M1 = np.array([0.0, 0.5, 1.0, 1.5, 2.0, 3.0, 4.0, 6.0, -0.0, -0.5, -1.0, -1.5, -2.0, -3.0, -4.0, -6.0])


def pack_weight(w, fmt):
    k, n = w.shape
    w = f64(bf(w)).reshape(k // 32, 32, n)
    amax = np.abs(w).max(1)
    if fmt == "e4m3":
        byte = np.frexp(amax)[1] - 1 + 127 - 7
    else:
        mant, ex = np.frexp(amax / 6.0)
        byte = np.where(mant > 0.5, ex, ex - 1) + 127
    byte = np.clip(np.where(amax > 0, byte, 1), 1, 254)
    scaled = (w * np.exp2(127.0 - byte)[:, None, :]).reshape(k, n).astype(np.float32)
    by_word = np.ascontiguousarray(scaled.reshape(k // 512, 128, 4, n).transpose(0, 1, 3, 2))
    if fmt == "e4m3":
        words = by_word.astype(ml_dtypes.float8_e4m3fn).view(np.uint8)
    else:
        c = by_word.astype(ml_dtypes.float4_e2m1fn).view(np.uint8) & 0xF
        words = c[..., 0::2] | (c[..., 1::2] << 4)
    return np.ascontiguousarray(words), np.ascontiguousarray(byte.astype(np.uint8).reshape(k // 512, 16, n))


def unpack_weight(words, scales, fmt):
    g, p, n, _ = words.shape
    if fmt == "e4m3":
        vals = np.ascontiguousarray(words).view(ml_dtypes.float8_e4m3fn).astype(np.float64)
    else:
        nib = np.empty((g, p, n, 4), np.uint8)
        nib[..., 0::2] = words & 0xF
        nib[..., 1::2] = words >> 4
        vals = E2M1[nib]
    vals = vals * np.repeat(np.exp2(scales.astype(np.float64) - 127.0), 8, axis=1)[..., None]
    return vals.transpose(0, 1, 3, 2).reshape(g * 512, n)

def pack4(w):
    words, scales = pack_weight(w, "e2m1")
    return words.reshape(words.shape[0], 128, -1), scales


def unpack4(words, scales):
    return unpack_weight(words.reshape(words.shape[0], 128, -1, 2), scales, "e2m1")


B, S, HID, H, KV, D, T = 1, 128, 16384, 16, 2, 128, 128
DQ = H * D
DKV = KV * D
OUT = DQ + 2 * DKV
THETA = 1e4


def make_pos_emb():
    i = np.repeat(np.arange(D // 2), 2)
    freq = np.power(THETA, -i * 2.0 / D)
    t = freq[:, None] * f64(np.arange(T))[None, :]
    cos = np.cos(t)
    sin = np.sin(t)
    sin[0::2] *= -1.0
    return np.concatenate([cos, sin], axis=0).T


def flip_pairs(x):
    return x.reshape(x.shape[:-1] + (D // 2, 2))[..., ::-1].reshape(x.shape)


def apply_rope(x, pe):
    return x * pe[:, :D] + flip_pairs(x) * pe[:, D:]


def setup_inputs():
    s = mx_kscale(HID)
    tensor = bf(np.random.standard_normal((B, S, HID)) * s)
    w = np.random.standard_normal((OUT, HID)) * 1.5 / np.sqrt(HID) / s[None, :]
    words, scales = pack4(np.ascontiguousarray(w.T))
    return {"tensor": tensor,
            "w_qkv_words": words,
            "w_qkv_scales": scales,
            "b_qkv": bf(np.random.standard_normal(OUT) * 0.3),
            "pos_emb": bf(make_pos_emb())}


def reference(tensor, w_qkv_words, w_qkv_scales, b_qkv, pos_emb):
    qkv = (mxq(f64(tensor), 2, "e4m3") @ unpack4(w_qkv_words, w_qkv_scales)) + f64(b_qkv)
    q = qkv[..., :DQ].reshape(B, S, H, D).transpose(0, 2, 1, 3)
    k = qkv[..., DQ:DQ + DKV].reshape(B, S, KV, D).transpose(0, 2, 1, 3)
    v = qkv[..., DQ + DKV:].reshape(B, S, KV, D).transpose(0, 2, 1, 3)
    pe = f64(pos_emb)[:S]
    return apply_rope(q, pe), apply_rope(k, pe), v

@@ -1,0 +1,230 @@
+from contextlib import ExitStack
+
+import concourse.mybir as mybir
+from concourse.masks import make_identity
+
+F32 = mybir.dt.float32
+BF16 = mybir.dt.bfloat16
+I32 = mybir.dt.int32
+U32 = mybir.dt.uint32
+U8 = mybir.dt.uint8
+FP8X4 = mybir.dt.float8_e4m3fn_x4
+FP4X4 = mybir.dt.float4_e2m1fn_x4
+ADD = mybir.AluOpType.add
+MULT = mybir.AluOpType.mult
+
+P = 128
+TOKENS = 128
+HID = 16384
+HEAD = 128
+Q_COLS = 16 * HEAD
+KV_COLS = 4 * HEAD
+OUT_COLS = Q_COLS + KV_COLS
+K_PASS = 4 * P
+PASSES = HID // K_PASS
+BANK = 512
+Q_BANKS = Q_COLS // BANK
+HEADS_PER_BANK = BANK // HEAD
+GROUP = 8
+GROUPS = PASSES // GROUP
+Q_CHUNK = 2
+KV_CHUNK = 2
+SCALE_RUN = 4
+
+FLOPS = 2 * TOKENS * HID * OUT_COLS
+
+
+def load_scale_rows(nc, plane, scale_words, first_pass):
+    for run in range(0, GROUP, SCALE_RUN):
+        for q in range(8):
+            partition = 32 * (q // 4) + q % 4
+            passes = slice(first_pass + run, first_pass + run + SCALE_RUN)
+            nc.sync.dma_start(
+                out=plane[partition:P:64, run : run + SCALE_RUN, :].bitcast(I32),
+                in_=scale_words[passes, q:16:8, :].rearrange("g q n -> q g n"),
+            )
+
+
+def quantise_tokens(nc, psum, stage, identity, x_raw, codes, scales):
+    x_words = x_raw[:].bitcast(F32)
+    grouped = stage.tile([P, GROUP, TOKENS, 4], BF16, align_bytes=64)
+    grouped_words = grouped[:].bitcast(F32)
+    for pair in range(0, GROUP, 2):
+        bank = psum.tile([P, BANK], F32, tag="work")
+        halves = bank[:].rearrange("p (i u m) -> p i u m", i=2, u=2)
+        for i in range(2):
+            first_word = (K_PASS // 2) * (pair + i)
+            for u in range(2):
+                nc.tensor.transpose(
+                    halves[:, i, u, :],
+                    x_words[:, first_word + u : first_word + K_PASS // 2 : 2],
+                    identity[:],
+                )
+        copy = nc.scalar.copy if pair % 4 == 0 else nc.vector.tensor_copy
+        copy(out=grouped_words[:, pair : pair + 2], in_=halves.rearrange("p i u m -> p i m u"))
+    nc.vector.quantize_mx(
+        out=codes[:].bitcast(FP8X4),
+        scales=scales[:],
+        in_=grouped[:].rearrange("p g m t -> p (g m t)"),
+    )
+
+
+def rope_and_store(nc, work, acc, bias, pos, heads, out_heads):
+    cols = heads * HEAD
+    pairs = HEAD // 2
+    x = work.tile([P, BANK], F32)
+    nc.vector.tensor_tensor(out=x[:, :cols], in0=acc, in1=bias, op=ADD)
+    by_head = x[:, :cols].rearrange("p (h d) -> p h d", h=heads)
+    by_pair = x[:, :cols].rearrange("p (h c e) -> p h c e", h=heads, e=2)
+
+    x_cos = work.tile([P, BANK], F32)
+    nc.vector.tensor_tensor(
+        out=x_cos[:, :cols].rearrange("p (h d) -> p h d", h=heads),
+        in0=by_head,
+        in1=pos[:, 0:HEAD].unsqueeze(1).to_broadcast([P, heads, HEAD]),
+        op=MULT,
+    )
+    sin = pos[:, HEAD : 2 * HEAD].rearrange("p (c e) -> p c e", e=2)
+    swapped_sin = work.tile([P, 2, BANK // 2], F32)
+    for e in range(2):
+        nc.vector.tensor_tensor(
+            out=swapped_sin[:, e, : cols // 2].rearrange("p (h c) -> p h c", h=heads),
+            in0=by_pair[:, :, :, 1 - e],
+            in1=sin[:, :, e].unsqueeze(1).to_broadcast([P, heads, pairs]),
+            op=MULT,
+        )
+    y = work.tile([P, BANK], F32)
+    nc.vector.tensor_tensor(
+        out=y[:, :cols].rearrange("p (j e) -> p j e", e=2),
+        in0=x_cos[:, :cols].rearrange("p (j e) -> p j e", e=2),
+        in1=swapped_sin[:, :, : cols // 2].rearrange("p e j -> p j e"),
+        op=ADD,
+    )
+    nc.scalar.dma_start(
+        out=out_heads.rearrange("h p d -> p h d"),
+        in_=y[:, :cols].rearrange("p (h d) -> p h d", h=heads),
+    )
+
+
+def tile_multiqueryattention_pa_k_kernel(
+    tc, tensor, w_qkv_words, w_qkv_scales, b_qkv, pos_emb, out_0, out_1, out_2
+):
+    nc = tc.nc
+    x_dram = tensor[0]
+    weight_words = w_qkv_words.bitcast(I32)
+    scale_words = w_qkv_scales.bitcast(I32)
+    q_ints = Q_COLS // 2
+
+    with ExitStack() as ctx:
+        keep = ctx.enter_context(tc.tile_pool(name="keep", bufs=1))
+        x_pool = ctx.enter_context(tc.tile_pool(name="x_raw", bufs=2))
+        stage = ctx.enter_context(tc.tile_pool(name="stage", bufs=2))
+        q_weights = ctx.enter_context(tc.tile_pool(name="q_weights", bufs=GROUP // Q_CHUNK))
+        kv_weights = ctx.enter_context(tc.tile_pool(name="kv_weights", bufs=8))
+        work = ctx.enter_context(tc.tile_pool(name="work", bufs=2))
+        acc_pool = ctx.enter_context(tc.psum_pool(name="acc", bufs=1))
+        psum = ctx.enter_context(tc.psum_pool(name="psum", bufs=3))
+        ctx.enter_context(tc.manual_schedule())
+
+        pos = keep.tile([P, 2 * HEAD], BF16)
+        nc.scalar.dma_start(out=pos[:], in_=pos_emb)
+        identity = keep.tile([P, P], F32)
+        make_identity(nc, identity[:])
+
+        bias_rows = keep.tile([P, OUT_COLS], BF16)
+        nc.vector.memset(bias_rows[:], 0.0)
+        nc.scalar.dma_start(out=bias_rows[0:1, :], in_=b_qkv.unsqueeze(0))
+        ones = keep.tile([P, P], BF16)
+        nc.vector.memset(ones[:], 1.0)
+        bias = keep.tile([P, OUT_COLS], F32)
+        for cols in range(0, OUT_COLS, BANK):
+            spread = psum.tile([P, BANK], F32, tag="work")
+            nc.tensor.matmul(
+                out=spread[:], lhsT=ones[:], rhs=bias_rows[:, cols : cols + BANK], start=True, stop=True
+            )
+            nc.scalar.copy(out=bias[:, cols : cols + BANK], in_=spread[:])
+
+        acc = [acc_pool.tile([P, BANK], F32, name="acc%d" % j) for j in range(Q_BANKS + 1)]
+        planes = []
+        x_codes = []
+        x_scales = []
+
+        for group in range(GROUPS):
+            first_pass = GROUP * group
+            x_raw = x_pool.tile([P, GROUP * K_PASS], BF16)
+            nc.sync.dma_start(
+                out=x_raw[:], in_=x_dram[:, K_PASS * first_pass : K_PASS * (first_pass + GROUP)]
+            )
+            plane = keep.tile([P, GROUP, OUT_COLS], U8, name="plane%d" % group, align_bytes=64)
+            nc.vector.memset(plane[:].rearrange("p g n -> p (g n)").bitcast(I32), 0)
+            load_scale_rows(nc, plane, scale_words, first_pass)
+            planes.append(plane)
+
+            chunks = []
+            for first in range(first_pass, first_pass + GROUP, Q_CHUNK):
+                words = q_weights.tile([P, Q_CHUNK, 2 * Q_COLS], U8, align_bytes=64)
+                nc.sync.dma_start(
+                    out=words[:].bitcast(I32),
+                    in_=weight_words[first : first + Q_CHUNK, :, 0:q_ints].rearrange("g p w -> p g w"),
+                )
+                chunks.append(words)
+
+            codes = keep.tile([P, GROUP * TOKENS], U32, name="x_codes%d" % group, align_bytes=64)
+            scales = keep.tile([P, GROUP * TOKENS], U8, name="x_scales%d" % group, align_bytes=64)
+            quantise_tokens(nc, psum, stage, identity, x_raw, codes, scales)
+            x_codes.append(codes)
+            x_scales.append(scales)
+
+            for i in range(GROUP):
+                tokens = slice(TOKENS * i, TOKENS * (i + 1))
+                words = chunks[i // Q_CHUNK]
+                for j in range(Q_BANKS):
+                    nc.tensor.matmul_mx(
+                        out=acc[j][:],
+                        lhsT=codes[:, tokens].bitcast(FP8X4),
+                        lhsT_scale=scales[:, tokens],
+                        rhs=words[:, i % Q_CHUNK, 2 * BANK * j : 2 * BANK * (j + 1)].bitcast(FP4X4),
+                        rhs_scale=plane[:, i, BANK * j : BANK * (j + 1)],
+                        start=(first_pass + i == 0),
+                        stop=(first_pass + i == PASSES - 1),
+                    )
+
+        for j in range(Q_BANKS):
+            rope_and_store(
+                nc,
+                work,
+                acc[j][:],
+                bias[:, BANK * j : BANK * (j + 1)],
+                pos,
+                HEADS_PER_BANK,
+                out_0[0, HEADS_PER_BANK * j : HEADS_PER_BANK * (j + 1)],
+            )
+
+        kv_acc = acc[Q_BANKS]
+        for first in range(0, PASSES, KV_CHUNK):
+            words = kv_weights.tile([P, KV_CHUNK, 2 * KV_COLS], U8, align_bytes=64)
+            nc.sync.dma_start(
+                out=words[:].bitcast(I32),
+                in_=weight_words[first : first + KV_CHUNK, :, q_ints:].rearrange("g p w -> p g w"),
+            )
+            for g in range(first, first + KV_CHUNK):
+                tokens = slice(TOKENS * (g % GROUP), TOKENS * (g % GROUP + 1))
+                nc.tensor.matmul_mx(
+                    out=kv_acc[:],
+                    lhsT=x_codes[g // GROUP][:, tokens].bitcast(FP8X4),
+                    lhsT_scale=x_scales[g // GROUP][:, tokens],
+                    rhs=words[:, g - first, :].bitcast(FP4X4),
+                    rhs_scale=planes[g // GROUP][:, g % GROUP, Q_COLS:OUT_COLS],
+                    start=(g == 0),
+                    stop=(g == PASSES - 1),
+                )
+
+        k_cols = 2 * HEAD
+        values = work.tile([P, k_cols], F32)
+        nc.vector.tensor_tensor(
+            out=values[:], in0=kv_acc[:, k_cols:], in1=bias[:, Q_COLS + k_cols :], op=ADD
+        )
+        nc.scalar.dma_start(
+            out=out_2[0].rearrange("h p d -> p h d"), in_=values[:].rearrange("p (h d) -> p h d", h=2)
+        )
+        rope_and_store(nc, work, kv_acc[:, :k_cols], bias[:, Q_COLS : Q_COLS + k_cols], pos, 2, out_1[0])

@@ -69,7 +69,7 @@ def quantise_tokens(nc, psum, stage, identity, x_raw, codes, scales):
     )
 
 
-def rope_and_store(nc, work, acc, bias, pos, heads, out_heads):
+def rope(nc, work, results, acc, bias, pos, heads):
     cols = heads * HEAD
     pairs = HEAD // 2
     x = work.tile([P, BANK], F32)
@@ -93,16 +93,20 @@ def rope_and_store(nc, work, acc, bias, pos, heads, out_heads):
             in1=sin[:, :, e].unsqueeze(1).to_broadcast([P, heads, pairs]),
             op=MULT,
         )
-    y = work.tile([P, BANK], F32)
+    y = results.tile([P, BANK], F32)
     nc.vector.tensor_tensor(
         out=y[:, :cols].rearrange("p (j e) -> p j e", e=2),
         in0=x_cos[:, :cols].rearrange("p (j e) -> p j e", e=2),
         in1=swapped_sin[:, :, : cols // 2].rearrange("p e j -> p j e"),
         op=ADD,
     )
-    nc.scalar.dma_start(
+    return y
+
+
+def store_heads(nc, out_heads, rows):
+    nc.sync.dma_start(
         out=out_heads.rearrange("h p d -> p h d"),
-        in_=y[:, :cols].rearrange("p (h d) -> p h d", h=heads),
+        in_=rows.rearrange("p (h d) -> p h d", d=HEAD),
     )
 
 
@@ -122,6 +126,7 @@ def tile_multiqueryattention_pa_k_kernel(
         q_weights = ctx.enter_context(tc.tile_pool(name="q_weights", bufs=GROUP // Q_CHUNK))
         kv_weights = ctx.enter_context(tc.tile_pool(name="kv_weights", bufs=8))
         work = ctx.enter_context(tc.tile_pool(name="work", bufs=2))
+        results = ctx.enter_context(tc.tile_pool(name="results", bufs=Q_BANKS + 1))
         acc_pool = ctx.enter_context(tc.psum_pool(name="acc", bufs=1))
         psum = ctx.enter_context(tc.psum_pool(name="psum", bufs=3))
         ctx.enter_context(tc.manual_schedule())
@@ -189,16 +194,10 @@ def tile_multiqueryattention_pa_k_kernel(
                         stop=(first_pass + i == PASSES - 1),
                     )
 
-        for j in range(Q_BANKS):
-            rope_and_store(
-                nc,
-                work,
-                acc[j][:],
-                bias[:, BANK * j : BANK * (j + 1)],
-                pos,
-                HEADS_PER_BANK,
-                out_0[0, HEADS_PER_BANK * j : HEADS_PER_BANK * (j + 1)],
-            )
+        queries = [
+            rope(nc, work, results, acc[j][:], bias[:, BANK * j : BANK * (j + 1)], pos, HEADS_PER_BANK)
+            for j in range(Q_BANKS)
+        ]
 
         kv_acc = acc[Q_BANKS]
         for first in range(0, PASSES, KV_CHUNK):
@@ -219,12 +218,13 @@ def tile_multiqueryattention_pa_k_kernel(
                     stop=(g == PASSES - 1),
                 )
 
+        for j in range(Q_BANKS):
+            store_heads(nc, out_0[0, HEADS_PER_BANK * j : HEADS_PER_BANK * (j + 1)], queries[j][:])
         k_cols = 2 * HEAD
         values = work.tile([P, k_cols], F32)
         nc.vector.tensor_tensor(
             out=values[:], in0=kv_acc[:, k_cols:], in1=bias[:, Q_COLS + k_cols :], op=ADD
         )
-        nc.scalar.dma_start(
-            out=out_2[0].rearrange("h p d -> p h d"), in_=values[:].rearrange("p (h d) -> p h d", h=2)
-        )
-        rope_and_store(nc, work, kv_acc[:, :k_cols], bias[:, Q_COLS : Q_COLS + k_cols], pos, 2, out_1[0])
+        store_heads(nc, out_2[0], values[:])
+        keys = rope(nc, work, results, kv_acc[:, :k_cols], bias[:, Q_COLS : Q_COLS + k_cols], pos, 2)
+        store_heads(nc, out_1[0], keys[:, :k_cols])

@@ -137,10 +137,73 @@ def tile_multiqueryattention_pa_k_kernel(
         make_identity(nc, identity[:])
 
         bias_rows = keep.tile([P, OUT_COLS], BF16)
-        nc.vector.memset(bias_rows[:], 0.0)
+        nc.gpsimd.memset(bias_rows[:], 0.0)
         nc.scalar.dma_start(out=bias_rows[0:1, :], in_=b_qkv.unsqueeze(0))
         ones = keep.tile([P, P], BF16)
-        nc.vector.memset(ones[:], 1.0)
+        nc.gpsimd.memset(ones[:], 1.0)
+
+        acc = [acc_pool.tile([P, BANK], F32, name="acc%d" % j) for j in range(Q_BANKS + 1)]
+        planes = []
+        x_codes = []
+        x_scales = []
+
+        chunks = []
+        x_tiles = []
+
+        def load_tokens(group):
+            x_raw = x_pool.tile([P, GROUP * K_PASS], BF16)
+            nc.sync.dma_start(
+                out=x_raw[:], in_=x_dram[:, GROUP * K_PASS * group : GROUP * K_PASS * (group + 1)]
+            )
+            x_tiles.append(x_raw)
+
+        def make_plane(group):
+            plane = keep.tile([P, GROUP, OUT_COLS], U8, name="plane%d" % group, align_bytes=64)
+            nc.vector.memset(plane[:].rearrange("p g n -> p (g n)").bitcast(I32), 0)
+            planes.append(plane)
+
+        def load_chunk(first):
+            words = q_weights.tile([P, Q_CHUNK, 2 * Q_COLS], U8, align_bytes=64)
+            nc.sync.dma_start(
+                out=words[:].bitcast(I32),
+                in_=weight_words[first : first + Q_CHUNK, :, 0:q_ints].rearrange("g p w -> p g w"),
+            )
+            chunks.append(words)
+
+        def quantise(group):
+            codes = keep.tile([P, GROUP * TOKENS], U32, name="x_codes%d" % group, align_bytes=64)
+            scales = keep.tile([P, GROUP * TOKENS], U8, name="x_scales%d" % group, align_bytes=64)
+            quantise_tokens(nc, psum, stage, identity, x_tiles[group], codes, scales)
+            x_codes.append(codes)
+            x_scales.append(scales)
+
+        load_tokens(0)
+        make_plane(0)
+        quantise(0)
+        for group in range(1, GROUPS):
+            make_plane(group)
+
+        for group in range(GROUPS):
+            first_pass = GROUP * group
+            load_scale_rows(nc, planes[group], scale_words, first_pass)
+            for first in range(first_pass, first_pass + GROUP, Q_CHUNK):
+                load_chunk(first)
+                if first == first_pass + GROUP // 2 and group + 1 < GROUPS:
+                    load_tokens(group + 1)
+                    quantise(group + 1)
+                for g in range(first, first + Q_CHUNK):
+                    tokens = slice(TOKENS * (g % GROUP), TOKENS * (g % GROUP + 1))
+                    for j in range(Q_BANKS):
+                        nc.tensor.matmul_mx(
+                            out=acc[j][:],
+                            lhsT=x_codes[group][:, tokens].bitcast(FP8X4),
+                            lhsT_scale=x_scales[group][:, tokens],
+                            rhs=chunks[-1][:, g - first, 2 * BANK * j : 2 * BANK * (j + 1)].bitcast(FP4X4),
+                            rhs_scale=planes[group][:, g % GROUP, BANK * j : BANK * (j + 1)],
+                            start=(g == 0),
+                            stop=(g == PASSES - 1),
+                        )
+
         bias = keep.tile([P, OUT_COLS], F32)
         for cols in range(0, OUT_COLS, BANK):
             spread = psum.tile([P, BANK], F32, tag="work")
@@ -148,51 +211,6 @@ def tile_multiqueryattention_pa_k_kernel(
                 out=spread[:], lhsT=ones[:], rhs=bias_rows[:, cols : cols + BANK], start=True, stop=True
             )
             nc.scalar.copy(out=bias[:, cols : cols + BANK], in_=spread[:])
-
-        acc = [acc_pool.tile([P, BANK], F32, name="acc%d" % j) for j in range(Q_BANKS + 1)]
-        planes = []
-        x_codes = []
-        x_scales = []
-
-        for group in range(GROUPS):
-            first_pass = GROUP * group
-            x_raw = x_pool.tile([P, GROUP * K_PASS], BF16)
-            nc.sync.dma_start(
-                out=x_raw[:], in_=x_dram[:, K_PASS * first_pass : K_PASS * (first_pass + GROUP)]
-            )
-            plane = keep.tile([P, GROUP, OUT_COLS], U8, name="plane%d" % group, align_bytes=64)
-            nc.vector.memset(plane[:].rearrange("p g n -> p (g n)").bitcast(I32), 0)
-            load_scale_rows(nc, plane, scale_words, first_pass)
-            planes.append(plane)
-
-            chunks = []
-            for first in range(first_pass, first_pass + GROUP, Q_CHUNK):
-                words = q_weights.tile([P, Q_CHUNK, 2 * Q_COLS], U8, align_bytes=64)
-                nc.sync.dma_start(
-                    out=words[:].bitcast(I32),
-                    in_=weight_words[first : first + Q_CHUNK, :, 0:q_ints].rearrange("g p w -> p g w"),
-                )
-                chunks.append(words)
-
-            codes = keep.tile([P, GROUP * TOKENS], U32, name="x_codes%d" % group, align_bytes=64)
-            scales = keep.tile([P, GROUP * TOKENS], U8, name="x_scales%d" % group, align_bytes=64)
-            quantise_tokens(nc, psum, stage, identity, x_raw, codes, scales)
-            x_codes.append(codes)
-            x_scales.append(scales)
-
-            for i in range(GROUP):
-                tokens = slice(TOKENS * i, TOKENS * (i + 1))
-                words = chunks[i // Q_CHUNK]
-                for j in range(Q_BANKS):
-                    nc.tensor.matmul_mx(
-                        out=acc[j][:],
-                        lhsT=codes[:, tokens].bitcast(FP8X4),
-                        lhsT_scale=scales[:, tokens],
-                        rhs=words[:, i % Q_CHUNK, 2 * BANK * j : 2 * BANK * (j + 1)].bitcast(FP4X4),
-                        rhs_scale=plane[:, i, BANK * j : BANK * (j + 1)],
-                        start=(first_pass + i == 0),
-                        stop=(first_pass + i == PASSES - 1),
-                    )
 
         queries = [
             rope(nc, work, results, acc[j][:], bias[:, BANK * j : BANK * (j + 1)], pos, HEADS_PER_BANK)

@@ -29,20 +29,18 @@ GROUP = 8
 GROUPS = PASSES // GROUP
 Q_CHUNK = 2
 KV_CHUNK = 2
-SCALE_RUN = 4
+PLANE = 16
 
 FLOPS = 2 * TOKENS * HID * OUT_COLS
 
 
 def load_scale_rows(nc, plane, scale_words, first_pass):
-    for run in range(0, GROUP, SCALE_RUN):
-        for q in range(8):
-            partition = 32 * (q // 4) + q % 4
-            passes = slice(first_pass + run, first_pass + run + SCALE_RUN)
-            nc.sync.dma_start(
-                out=plane[partition:P:64, run : run + SCALE_RUN, :].bitcast(I32),
-                in_=scale_words[passes, q:16:8, :].rearrange("g q n -> q g n"),
-            )
+    for q in range(8):
+        partition = 32 * (q // 4) + q % 4
+        nc.sync.dma_start(
+            out=plane[partition:P:64, :, :].bitcast(I32),
+            in_=scale_words[first_pass : first_pass + PLANE, q:16:8, :].rearrange("g q n -> q g n"),
+        )
 
 
 def quantise_tokens(nc, psum, stage, identity, x_raw, codes, scales):
@@ -121,9 +119,9 @@ def tile_multiqueryattention_pa_k_kernel(
 
     with ExitStack() as ctx:
         keep = ctx.enter_context(tc.tile_pool(name="keep", bufs=1))
-        x_pool = ctx.enter_context(tc.tile_pool(name="x_raw", bufs=2))
+        x_pool = ctx.enter_context(tc.tile_pool(name="x_raw", bufs=GROUPS))
         stage = ctx.enter_context(tc.tile_pool(name="stage", bufs=2))
-        q_weights = ctx.enter_context(tc.tile_pool(name="q_weights", bufs=GROUP // Q_CHUNK))
+        q_weights = ctx.enter_context(tc.tile_pool(name="q_weights", bufs=4))
         kv_weights = ctx.enter_context(tc.tile_pool(name="kv_weights", bufs=8))
         work = ctx.enter_context(tc.tile_pool(name="work", bufs=2))
         results = ctx.enter_context(tc.tile_pool(name="results", bufs=Q_BANKS + 1))
@@ -157,11 +155,6 @@ def tile_multiqueryattention_pa_k_kernel(
             )
             x_tiles.append(x_raw)
 
-        def make_plane(group):
-            plane = keep.tile([P, GROUP, OUT_COLS], U8, name="plane%d" % group, align_bytes=64)
-            nc.vector.memset(plane[:].rearrange("p g n -> p (g n)").bitcast(I32), 0)
-            planes.append(plane)
-
         def load_chunk(first):
             words = q_weights.tile([P, Q_CHUNK, 2 * Q_COLS], U8, align_bytes=64)
             nc.sync.dma_start(
@@ -170,6 +163,18 @@ def tile_multiqueryattention_pa_k_kernel(
             )
             chunks.append(words)
 
+        def multiply(g, j, words):
+            tokens = slice(TOKENS * (g % GROUP), TOKENS * (g % GROUP + 1))
+            nc.tensor.matmul_mx(
+                out=acc[j][:],
+                lhsT=x_codes[g // GROUP][:, tokens].bitcast(FP8X4),
+                lhsT_scale=x_scales[g // GROUP][:, tokens],
+                rhs=words.bitcast(FP4X4),
+                rhs_scale=planes[g // PLANE][:, g % PLANE, BANK * j : BANK * (j + 1)],
+                start=(g == 0),
+                stop=(g == PASSES - 1),
+            )
+
         def quantise(group):
             codes = keep.tile([P, GROUP * TOKENS], U32, name="x_codes%d" % group, align_bytes=64)
             scales = keep.tile([P, GROUP * TOKENS], U8, name="x_scales%d" % group, align_bytes=64)
@@ -177,40 +182,30 @@ def tile_multiqueryattention_pa_k_kernel(
             x_codes.append(codes)
             x_scales.append(scales)
 
-        load_tokens(0)
-        make_plane(0)
-        quantise(0)
-        for group in range(1, GROUPS):
-            make_plane(group)
-
+        for first in range(0, PASSES, PLANE):
+            plane = keep.tile([P, PLANE, OUT_COLS], U8, name="plane%d" % first, align_bytes=64)
+            nc.vector.memset(plane[:].rearrange("p g n -> p (g n)").bitcast(I32), 0)
+            planes.append(plane)
         for group in range(GROUPS):
-            first_pass = GROUP * group
-            load_scale_rows(nc, planes[group], scale_words, first_pass)
-            for first in range(first_pass, first_pass + GROUP, Q_CHUNK):
-                load_chunk(first)
-                if first == first_pass + GROUP // 2 and group + 1 < GROUPS:
-                    load_tokens(group + 1)
-                    quantise(group + 1)
-                for g in range(first, first + Q_CHUNK):
-                    tokens = slice(TOKENS * (g % GROUP), TOKENS * (g % GROUP + 1))
-                    for j in range(Q_BANKS):
-                        nc.tensor.matmul_mx(
-                            out=acc[j][:],
-                            lhsT=x_codes[group][:, tokens].bitcast(FP8X4),
-                            lhsT_scale=x_scales[group][:, tokens],
-                            rhs=chunks[-1][:, g - first, 2 * BANK * j : 2 * BANK * (j + 1)].bitcast(FP4X4),
-                            rhs_scale=planes[group][:, g % GROUP, BANK * j : BANK * (j + 1)],
-                            start=(g == 0),
-                            stop=(g == PASSES - 1),
-                        )
+            load_tokens(group)
+        for half, plane in enumerate(planes):
+            load_scale_rows(nc, plane, scale_words, PLANE * half)
+        for group in range(GROUPS):
+            quantise(group)
 
-        bias = keep.tile([P, OUT_COLS], F32)
+        bias = keep.tile([P, OUT_COLS], BF16)
         for cols in range(0, OUT_COLS, BANK):
             spread = psum.tile([P, BANK], F32, tag="work")
             nc.tensor.matmul(
                 out=spread[:], lhsT=ones[:], rhs=bias_rows[:, cols : cols + BANK], start=True, stop=True
             )
             nc.scalar.copy(out=bias[:, cols : cols + BANK], in_=spread[:])
+
+        for first in range(0, PASSES, Q_CHUNK):
+            load_chunk(first)
+            for g in range(first, first + Q_CHUNK):
+                for j in range(Q_BANKS):
+                    multiply(g, j, chunks[-1][:, g - first, 2 * BANK * j : 2 * BANK * (j + 1)])
 
         queries = [
             rope(nc, work, results, acc[j][:], bias[:, BANK * j : BANK * (j + 1)], pos, HEADS_PER_BANK)
@@ -225,16 +220,7 @@ def tile_multiqueryattention_pa_k_kernel(
                 in_=weight_words[first : first + KV_CHUNK, :, q_ints:].rearrange("g p w -> p g w"),
             )
             for g in range(first, first + KV_CHUNK):
-                tokens = slice(TOKENS * (g % GROUP), TOKENS * (g % GROUP + 1))
-                nc.tensor.matmul_mx(
-                    out=kv_acc[:],
-                    lhsT=x_codes[g // GROUP][:, tokens].bitcast(FP8X4),
-                    lhsT_scale=x_scales[g // GROUP][:, tokens],
-                    rhs=words[:, g - first, :].bitcast(FP4X4),
-                    rhs_scale=planes[g // GROUP][:, g % GROUP, Q_COLS:OUT_COLS],
-                    start=(g == 0),
-                    stop=(g == PASSES - 1),
-                )
+                multiply(g, Q_BANKS, words[:, g - first, :])
 
         for j in range(Q_BANKS):
             store_heads(nc, out_0[0, HEADS_PER_BANK * j : HEADS_PER_BANK * (j + 1)], queries[j][:])

@@ -34,12 +34,13 @@ PLANE = 16
 FLOPS = 2 * TOKENS * HID * OUT_COLS
 
 
-def load_scale_rows(nc, plane, scale_words, first_pass):
+def load_scale_rows(nc, plane, scale_words, passes, cols):
+    ints = slice(cols.start // 4, cols.stop // 4)
     for q in range(8):
         partition = 32 * (q // 4) + q % 4
         nc.sync.dma_start(
             out=plane[partition:P:64, :, :].bitcast(I32),
-            in_=scale_words[first_pass : first_pass + PLANE, q:16:8, :].rearrange("g q n -> q g n"),
+            in_=scale_words[passes, q:16:8, ints].rearrange("g q n -> q g n"),
         )
 
 
@@ -163,14 +164,14 @@ def tile_multiqueryattention_pa_k_kernel(
             )
             chunks.append(words)
 
-        def multiply(g, j, words):
+        def multiply(g, j, words, plane):
             tokens = slice(TOKENS * (g % GROUP), TOKENS * (g % GROUP + 1))
             nc.tensor.matmul_mx(
                 out=acc[j][:],
                 lhsT=x_codes[g // GROUP][:, tokens].bitcast(FP8X4),
                 lhsT_scale=x_scales[g // GROUP][:, tokens],
                 rhs=words.bitcast(FP4X4),
-                rhs_scale=planes[g // PLANE][:, g % PLANE, BANK * j : BANK * (j + 1)],
+                rhs_scale=plane,
                 start=(g == 0),
                 stop=(g == PASSES - 1),
             )
@@ -182,14 +183,19 @@ def tile_multiqueryattention_pa_k_kernel(
             x_codes.append(codes)
             x_scales.append(scales)
 
-        for first in range(0, PASSES, PLANE):
-            plane = keep.tile([P, PLANE, OUT_COLS], U8, name="plane%d" % first, align_bytes=64)
+        def make_plane(passes, cols, name):
+            plane = keep.tile([P, passes, cols], U8, name=name, align_bytes=64)
             nc.vector.memset(plane[:].rearrange("p g n -> p (g n)").bitcast(I32), 0)
-            planes.append(plane)
+            return plane
+
         for group in range(GROUPS):
             load_tokens(group)
-        for half, plane in enumerate(planes):
-            load_scale_rows(nc, plane, scale_words, PLANE * half)
+        for first in range(0, PASSES, PLANE):
+            plane = make_plane(PLANE, Q_COLS, "plane%d" % first)
+            load_scale_rows(nc, plane, scale_words, slice(first, first + PLANE), slice(0, Q_COLS))
+            planes.append(plane)
+        kv_plane = make_plane(PASSES, KV_COLS, "kv_plane")
+        load_scale_rows(nc, kv_plane, scale_words, slice(0, PASSES), slice(Q_COLS, OUT_COLS))
         for group in range(GROUPS):
             quantise(group)
 
@@ -205,7 +211,12 @@ def tile_multiqueryattention_pa_k_kernel(
             load_chunk(first)
             for g in range(first, first + Q_CHUNK):
                 for j in range(Q_BANKS):
-                    multiply(g, j, chunks[-1][:, g - first, 2 * BANK * j : 2 * BANK * (j + 1)])
+                    multiply(
+                        g,
+                        j,
+                        chunks[-1][:, g - first, 2 * BANK * j : 2 * BANK * (j + 1)],
+                        planes[g // PLANE][:, g % PLANE, BANK * j : BANK * (j + 1)],
+                    )
 
         queries = [
             rope(nc, work, results, acc[j][:], bias[:, BANK * j : BANK * (j + 1)], pos, HEADS_PER_BANK)
@@ -220,7 +231,7 @@ def tile_multiqueryattention_pa_k_kernel(
                 in_=weight_words[first : first + KV_CHUNK, :, q_ints:].rearrange("g p w -> p g w"),
             )
             for g in range(first, first + KV_CHUNK):
-                multiply(g, Q_BANKS, words[:, g - first, :])
+                multiply(g, Q_BANKS, words[:, g - first, :], kv_plane[:, g, :])
 
         for j in range(Q_BANKS):
             store_heads(nc, out_0[0, HEADS_PER_BANK * j : HEADS_PER_BANK * (j + 1)], queries[j][:])

@@ -36,12 +36,13 @@ FLOPS = 2 * TOKENS * HID * OUT_COLS
 
 def load_scale_rows(nc, plane, scale_words, passes, cols):
     ints = slice(cols.start // 4, cols.stop // 4)
-    for q in range(8):
-        partition = 32 * (q // 4) + q % 4
-        nc.sync.dma_start(
-            out=plane[partition:P:64, :, :].bitcast(I32),
-            in_=scale_words[passes, q:16:8, ints].rearrange("g q n -> q g n"),
-        )
+    for i in range(4):
+        for quadrant in (0, 2, 1, 3):
+            partition = 32 * quadrant + i
+            nc.sync.dma_start(
+                out=plane[partition : partition + 1, :, :].bitcast(I32),
+                in_=scale_words[passes, 4 * quadrant + i, ints].unsqueeze(0),
+            )
 
 
 def quantise_tokens(nc, psum, stage, identity, x_raw, codes, scales):

@@ -27,22 +27,19 @@ Q_BANKS = Q_COLS // BANK
 HEADS_PER_BANK = BANK // HEAD
 GROUP = 8
 GROUPS = PASSES // GROUP
+HALF = PASSES // 2
 Q_CHUNK = 2
-KV_CHUNK = 2
-PLANE = 16
+EARLY = 4
 
 FLOPS = 2 * TOKENS * HID * OUT_COLS
 
 
-def load_scale_rows(nc, plane, scale_words, passes, cols):
-    ints = slice(cols.start // 4, cols.stop // 4)
-    for i in range(4):
-        for quadrant in (0, 2, 1, 3):
-            partition = 32 * quadrant + i
-            nc.sync.dma_start(
-                out=plane[partition : partition + 1, :, :].bitcast(I32),
-                in_=scale_words[passes, 4 * quadrant + i, ints].unsqueeze(0),
-            )
+def scale_row_load(nc, plane, scale_words, passes, cols, row):
+    partition = 32 * (row // 4) + row % 4
+    nc.sync.dma_start(
+        out=plane[partition : partition + 1, :, :].bitcast(I32),
+        in_=scale_words[passes, row, cols.start // 4 : cols.stop // 4].unsqueeze(0),
+    )
 
 
 def quantise_tokens(nc, psum, stage, identity, x_raw, codes, scales):
@@ -69,35 +66,21 @@ def quantise_tokens(nc, psum, stage, identity, x_raw, codes, scales):
     )
 
 
-def rope(nc, work, results, acc, bias, pos, heads):
-    cols = heads * HEAD
-    pairs = HEAD // 2
-    x = work.tile([P, BANK], F32)
-    nc.vector.tensor_tensor(out=x[:, :cols], in0=acc, in1=bias, op=ADD)
-    by_head = x[:, :cols].rearrange("p (h d) -> p h d", h=heads)
-    by_pair = x[:, :cols].rearrange("p (h c e) -> p h c e", h=heads, e=2)
-
-    x_cos = work.tile([P, BANK], F32)
+def rope(nc, work, results, x, coefficients, heads):
+    products = work.tile([P, 2, BANK], F32)
+    shape = [P, 2, heads, HEAD]
     nc.vector.tensor_tensor(
-        out=x_cos[:, :cols].rearrange("p (h d) -> p h d", h=heads),
-        in0=by_head,
-        in1=pos[:, 0:HEAD].unsqueeze(1).to_broadcast([P, heads, HEAD]),
+        out=products[:, :, : heads * HEAD].rearrange("p s (h d) -> p s h d", h=heads),
+        in0=x.rearrange("p (h d) -> p h d", h=heads).unsqueeze(1).to_broadcast(shape),
+        in1=coefficients[:].unsqueeze(2).to_broadcast(shape),
         op=MULT,
     )
-    sin = pos[:, HEAD : 2 * HEAD].rearrange("p (c e) -> p c e", e=2)
-    swapped_sin = work.tile([P, 2, BANK // 2], F32)
-    for e in range(2):
-        nc.vector.tensor_tensor(
-            out=swapped_sin[:, e, : cols // 2].rearrange("p (h c) -> p h c", h=heads),
-            in0=by_pair[:, :, :, 1 - e],
-            in1=sin[:, :, e].unsqueeze(1).to_broadcast([P, heads, pairs]),
-            op=MULT,
-        )
+    by_pair = products[:, :, : heads * HEAD].rearrange("p s (j e) -> p s j e", e=2)
     y = results.tile([P, BANK], F32)
     nc.vector.tensor_tensor(
-        out=y[:, :cols].rearrange("p (j e) -> p j e", e=2),
-        in0=x_cos[:, :cols].rearrange("p (j e) -> p j e", e=2),
-        in1=swapped_sin[:, :, : cols // 2].rearrange("p e j -> p j e"),
+        out=y[:, : heads * HEAD].rearrange("p (j e) -> p j e", e=2),
+        in0=by_pair[:, 0],
+        in1=by_pair[:, 1, :, ::-1],
         op=ADD,
     )
     return y
@@ -121,49 +104,34 @@ def tile_multiqueryattention_pa_k_kernel(
 
     with ExitStack() as ctx:
         keep = ctx.enter_context(tc.tile_pool(name="keep", bufs=1))
-        x_pool = ctx.enter_context(tc.tile_pool(name="x_raw", bufs=GROUPS))
+        group_pool = ctx.enter_context(tc.tile_pool(name="groups", bufs=GROUPS))
         stage = ctx.enter_context(tc.tile_pool(name="stage", bufs=2))
-        q_weights = ctx.enter_context(tc.tile_pool(name="q_weights", bufs=4))
-        kv_weights = ctx.enter_context(tc.tile_pool(name="kv_weights", bufs=8))
+        q_weights = ctx.enter_context(tc.tile_pool(name="q_weights", bufs=6))
         work = ctx.enter_context(tc.tile_pool(name="work", bufs=2))
         results = ctx.enter_context(tc.tile_pool(name="results", bufs=Q_BANKS + 1))
         acc_pool = ctx.enter_context(tc.psum_pool(name="acc", bufs=1))
         psum = ctx.enter_context(tc.psum_pool(name="psum", bufs=3))
         ctx.enter_context(tc.manual_schedule())
 
-        pos = keep.tile([P, 2 * HEAD], BF16)
-        nc.scalar.dma_start(out=pos[:], in_=pos_emb)
-        identity = keep.tile([P, P], F32)
-        make_identity(nc, identity[:])
-
-        bias_rows = keep.tile([P, OUT_COLS], BF16)
-        nc.gpsimd.memset(bias_rows[:], 0.0)
-        nc.scalar.dma_start(out=bias_rows[0:1, :], in_=b_qkv.unsqueeze(0))
-        ones = keep.tile([P, P], BF16)
-        nc.gpsimd.memset(ones[:], 1.0)
-
         acc = [acc_pool.tile([P, BANK], F32, name="acc%d" % j) for j in range(Q_BANKS + 1)]
         planes = []
         x_codes = []
         x_scales = []
+        q_chunks = []
 
-        chunks = []
-        x_tiles = []
-
-        def load_tokens(group):
-            x_raw = x_pool.tile([P, GROUP * K_PASS], BF16)
-            nc.sync.dma_start(
-                out=x_raw[:], in_=x_dram[:, GROUP * K_PASS * group : GROUP * K_PASS * (group + 1)]
-            )
-            x_tiles.append(x_raw)
-
-        def load_chunk(first):
-            words = q_weights.tile([P, Q_CHUNK, 2 * Q_COLS], U8, align_bytes=64)
+        def load_q_weights():
+            first = Q_CHUNK * len(q_chunks)
+            words = q_weights.tile([P, Q_CHUNK, 2 * Q_COLS], U8, align_bytes=256)
             nc.sync.dma_start(
                 out=words[:].bitcast(I32),
                 in_=weight_words[first : first + Q_CHUNK, :, 0:q_ints].rearrange("g p w -> p g w"),
             )
-            chunks.append(words)
+            q_chunks.append(words)
+
+        def make_plane(passes, cols, name):
+            plane = keep.tile([P, passes, cols], U8, name=name, align_bytes=256)
+            nc.vector.memset(plane[:].rearrange("p g n -> p (g n)").bitcast(I32), 0)
+            return plane
 
         def multiply(g, j, words, plane):
             tokens = slice(TOKENS * (g % GROUP), TOKENS * (g % GROUP + 1))
@@ -177,28 +145,57 @@ def tile_multiqueryattention_pa_k_kernel(
                 stop=(g == PASSES - 1),
             )
 
-        def quantise(group):
+        def multiply_queries(chunk):
+            for i in range(Q_CHUNK):
+                g = Q_CHUNK * chunk + i
+                for j in range(Q_BANKS):
+                    multiply(
+                        g,
+                        j,
+                        q_chunks[chunk][:, i, 2 * BANK * j : 2 * BANK * (j + 1)],
+                        planes[g // HALF][:, g % HALF, BANK * j : BANK * (j + 1)],
+                    )
+
+        x_tiles = []
+
+        def load_tokens(group):
+            x_raw = group_pool.tile([P, GROUP * K_PASS], BF16, tag="group", align_bytes=256)
+            nc.sync.dma_start(
+                out=x_raw[:], in_=x_dram[:, GROUP * K_PASS * group : GROUP * K_PASS * (group + 1)]
+            )
+            x_tiles.append(x_raw)
+
+        load_tokens(0)
+        for chunk in range(EARLY):
+            load_q_weights()
+        for group in range(1, GROUPS):
+            load_tokens(group)
+
+        rows = [4 * quadrant + i for i in range(4) for quadrant in (0, 2, 1, 3)]
+        for first in range(0, PASSES, HALF):
+            planes.append(make_plane(HALF, Q_COLS, "plane%d" % first))
+            for row in rows:
+                scale_row_load(nc, planes[-1], scale_words, slice(first, first + HALF), slice(0, Q_COLS), row)
+        kv_plane = make_plane(PASSES, KV_COLS, "kv_plane")
+        for row in rows:
+            scale_row_load(nc, kv_plane, scale_words, slice(0, PASSES), slice(Q_COLS, OUT_COLS), row)
+
+        identity = keep.tile([P, P], F32)
+        make_identity(nc, identity[:])
+        bias_rows = keep.tile([P, OUT_COLS], BF16)
+        nc.gpsimd.memset(bias_rows[:], 0.0)
+        nc.scalar.dma_start(out=bias_rows[0:1, :], in_=b_qkv.unsqueeze(0))
+        ones = keep.tile([P, P], BF16)
+        nc.gpsimd.memset(ones[:], 1.0)
+        pos = keep.tile([P, 2 * HEAD], BF16)
+        nc.scalar.dma_start(out=pos[:], in_=pos_emb)
+
+        for group in range(GROUPS):
             codes = keep.tile([P, GROUP * TOKENS], U32, name="x_codes%d" % group, align_bytes=64)
             scales = keep.tile([P, GROUP * TOKENS], U8, name="x_scales%d" % group, align_bytes=64)
             quantise_tokens(nc, psum, stage, identity, x_tiles[group], codes, scales)
             x_codes.append(codes)
             x_scales.append(scales)
-
-        def make_plane(passes, cols, name):
-            plane = keep.tile([P, passes, cols], U8, name=name, align_bytes=64)
-            nc.vector.memset(plane[:].rearrange("p g n -> p (g n)").bitcast(I32), 0)
-            return plane
-
-        for group in range(GROUPS):
-            load_tokens(group)
-        for first in range(0, PASSES, PLANE):
-            plane = make_plane(PLANE, Q_COLS, "plane%d" % first)
-            load_scale_rows(nc, plane, scale_words, slice(first, first + PLANE), slice(0, Q_COLS))
-            planes.append(plane)
-        kv_plane = make_plane(PASSES, KV_COLS, "kv_plane")
-        load_scale_rows(nc, kv_plane, scale_words, slice(0, PASSES), slice(Q_COLS, OUT_COLS))
-        for group in range(GROUPS):
-            quantise(group)
 
         bias = keep.tile([P, OUT_COLS], BF16)
         for cols in range(0, OUT_COLS, BANK):
@@ -207,40 +204,42 @@ def tile_multiqueryattention_pa_k_kernel(
                 out=spread[:], lhsT=ones[:], rhs=bias_rows[:, cols : cols + BANK], start=True, stop=True
             )
             nc.scalar.copy(out=bias[:, cols : cols + BANK], in_=spread[:])
+        coefficients = keep.tile([P, 2, HEAD], BF16)
+        nc.vector.tensor_copy(out=coefficients[:, 0, :], in_=pos[:, :HEAD])
+        nc.vector.tensor_copy(
+            out=coefficients[:, 1, :].rearrange("p (c e) -> p c e", e=2),
+            in_=pos[:, HEAD:].rearrange("p (c e) -> p c e", e=2)[:, :, ::-1],
+        )
 
-        for first in range(0, PASSES, Q_CHUNK):
-            load_chunk(first)
-            for g in range(first, first + Q_CHUNK):
-                for j in range(Q_BANKS):
-                    multiply(
-                        g,
-                        j,
-                        chunks[-1][:, g - first, 2 * BANK * j : 2 * BANK * (j + 1)],
-                        planes[g // PLANE][:, g % PLANE, BANK * j : BANK * (j + 1)],
-                    )
-
-        queries = [
-            rope(nc, work, results, acc[j][:], bias[:, BANK * j : BANK * (j + 1)], pos, HEADS_PER_BANK)
-            for j in range(Q_BANKS)
-        ]
+        for chunk in range(PASSES // Q_CHUNK):
+            if chunk >= EARLY:
+                load_q_weights()
+            multiply_queries(chunk)
+        queries = []
+        for j in range(Q_BANKS):
+            x = work.tile([P, BANK], F32)
+            nc.vector.tensor_tensor(out=x[:], in0=acc[j][:], in1=bias[:, BANK * j : BANK * (j + 1)], op=ADD)
+            queries.append(rope(nc, work, results, x[:], coefficients, HEADS_PER_BANK))
 
         kv_acc = acc[Q_BANKS]
-        for first in range(0, PASSES, KV_CHUNK):
-            words = kv_weights.tile([P, KV_CHUNK, 2 * KV_COLS], U8, align_bytes=64)
-            nc.sync.dma_start(
-                out=words[:].bitcast(I32),
-                in_=weight_words[first : first + KV_CHUNK, :, q_ints:].rearrange("g p w -> p g w"),
-            )
-            for g in range(first, first + KV_CHUNK):
-                multiply(g, Q_BANKS, words[:, g - first, :], kv_plane[:, g, :])
+        for group in range(GROUPS):
+            words = group_pool.tile([P, GROUP, 2 * KV_COLS], U8, tag="group", align_bytes=256)
+            first = 0
+            for count in (8,) if group < GROUPS - 1 else (4, 2, 2):
+                g = GROUP * group + first
+                nc.sync.dma_start(
+                    out=words[:, first : first + count, :].bitcast(I32),
+                    in_=weight_words[g : g + count, :, q_ints:].rearrange("g p w -> p g w"),
+                )
+                for i in range(count):
+                    multiply(g + i, Q_BANKS, words[:, first + i, :], kv_plane[:, g + i, :])
+                first += count
 
         for j in range(Q_BANKS):
             store_heads(nc, out_0[0, HEADS_PER_BANK * j : HEADS_PER_BANK * (j + 1)], queries[j][:])
+        x = work.tile([P, BANK], F32)
+        nc.vector.tensor_tensor(out=x[:], in0=kv_acc[:], in1=bias[:, Q_COLS:], op=ADD)
         k_cols = 2 * HEAD
-        values = work.tile([P, k_cols], F32)
-        nc.vector.tensor_tensor(
-            out=values[:], in0=kv_acc[:, k_cols:], in1=bias[:, Q_COLS + k_cols :], op=ADD
-        )
-        store_heads(nc, out_2[0], values[:])
-        keys = rope(nc, work, results, kv_acc[:, :k_cols], bias[:, Q_COLS : Q_COLS + k_cols], pos, 2)
+        store_heads(nc, out_2[0], x[:, k_cols:])
+        keys = rope(nc, work, results, x[:, :k_cols], coefficients, 2)
         store_heads(nc, out_1[0], keys[:, :k_cols])

@@ -29,7 +29,7 @@ GROUP = 8
 GROUPS = PASSES // GROUP
 HALF = PASSES // 2
 Q_CHUNK = 2
-EARLY = 4
+EARLY = 6
 
 FLOPS = 2 * TOKENS * HID * OUT_COLS
 
@@ -146,9 +146,9 @@ def tile_multiqueryattention_pa_k_kernel(
             )
 
         def multiply_queries(chunk):
-            for i in range(Q_CHUNK):
-                g = Q_CHUNK * chunk + i
-                for j in range(Q_BANKS):
+            for j in range(Q_BANKS):
+                for i in range(Q_CHUNK):
+                    g = Q_CHUNK * chunk + i
                     multiply(
                         g,
                         j,
@@ -174,9 +174,11 @@ def tile_multiqueryattention_pa_k_kernel(
         rows = [4 * quadrant + i for i in range(4) for quadrant in (0, 2, 1, 3)]
         for first in range(0, PASSES, HALF):
             planes.append(make_plane(HALF, Q_COLS, "plane%d" % first))
-            for row in rows:
-                scale_row_load(nc, planes[-1], scale_words, slice(first, first + HALF), slice(0, Q_COLS), row)
         kv_plane = make_plane(PASSES, KV_COLS, "kv_plane")
+        for row in rows:
+            scale_row_load(nc, planes[0], scale_words, slice(0, HALF), slice(0, Q_COLS), row)
+        for row in rows:
+            scale_row_load(nc, planes[1], scale_words, slice(HALF, PASSES), slice(0, Q_COLS), row)
         for row in rows:
             scale_row_load(nc, kv_plane, scale_words, slice(0, PASSES), slice(Q_COLS, OUT_COLS), row)
 
@@ -225,7 +227,7 @@ def tile_multiqueryattention_pa_k_kernel(
         for group in range(GROUPS):
             words = group_pool.tile([P, GROUP, 2 * KV_COLS], U8, tag="group", align_bytes=256)
             first = 0
-            for count in (8,) if group < GROUPS - 1 else (4, 2, 2):
+            for count in (8,) if group < GROUPS - 1 else (4, 2, 1, 1):
                 g = GROUP * group + first
                 nc.sync.dma_start(
                     out=words[:, first : first + count, :].bitcast(I32),
@@ -237,9 +239,12 @@ def tile_multiqueryattention_pa_k_kernel(
 
         for j in range(Q_BANKS):
             store_heads(nc, out_0[0, HEADS_PER_BANK * j : HEADS_PER_BANK * (j + 1)], queries[j][:])
-        x = work.tile([P, BANK], F32)
-        nc.vector.tensor_tensor(out=x[:], in0=kv_acc[:], in1=bias[:, Q_COLS:], op=ADD)
         k_cols = 2 * HEAD
+        x = work.tile([P, BANK], F32)
+        for cols in (slice(0, k_cols), slice(k_cols, KV_COLS)):
+            nc.vector.tensor_tensor(
+                out=x[:, cols], in0=kv_acc[:, cols], in1=bias[:, Q_COLS + cols.start : Q_COLS + cols.stop], op=ADD
+            )
         store_heads(nc, out_2[0], x[:, k_cols:])
         keys = rope(nc, work, results, x[:, :k_cols], coefficients, 2)
         store_heads(nc, out_1[0], keys[:, :k_cols])

from contextlib import ExitStack

import concourse.mybir as mybir
from concourse.masks import make_identity

F32 = mybir.dt.float32
BF16 = mybir.dt.bfloat16
I32 = mybir.dt.int32
U32 = mybir.dt.uint32
U8 = mybir.dt.uint8
FP8X4 = mybir.dt.float8_e4m3fn_x4
FP4X4 = mybir.dt.float4_e2m1fn_x4
ADD = mybir.AluOpType.add
MULT = mybir.AluOpType.mult

P = 128
TOKENS = 128
HID = 16384
HEAD = 128
Q_COLS = 16 * HEAD
KV_COLS = 4 * HEAD
OUT_COLS = Q_COLS + KV_COLS
K_PASS = 4 * P
PASSES = HID // K_PASS
BANK = 512
Q_BANKS = Q_COLS // BANK
HEADS_PER_BANK = BANK // HEAD
GROUP = 8
GROUPS = PASSES // GROUP
HALF = PASSES // 2
Q_CHUNK = 2
EARLY = 6

FLOPS = 2 * TOKENS * HID * OUT_COLS


def scale_row_load(nc, plane, scale_words, passes, cols, row):
    partition = 32 * (row // 4) + row % 4
    nc.sync.dma_start(
        out=plane[partition : partition + 1, :, :].bitcast(I32),
        in_=scale_words[passes, row, cols.start // 4 : cols.stop // 4].unsqueeze(0),
    )


def quantise_tokens(nc, psum, stage, identity, x_raw, codes, scales):
    x_words = x_raw[:].bitcast(F32)
    grouped = stage.tile([P, GROUP, TOKENS, 4], BF16, align_bytes=64)
    grouped_words = grouped[:].bitcast(F32)
    for pair in range(0, GROUP, 2):
        bank = psum.tile([P, BANK], F32, tag="work")
        halves = bank[:].rearrange("p (i u m) -> p i u m", i=2, u=2)
        for i in range(2):
            first_word = (K_PASS // 2) * (pair + i)
            for u in range(2):
                nc.tensor.transpose(
                    halves[:, i, u, :],
                    x_words[:, first_word + u : first_word + K_PASS // 2 : 2],
                    identity[:],
                )
        copy = nc.scalar.copy if pair % 4 == 0 else nc.vector.tensor_copy
        copy(out=grouped_words[:, pair : pair + 2], in_=halves.rearrange("p i u m -> p i m u"))
    nc.vector.quantize_mx(
        out=codes[:].bitcast(FP8X4),
        scales=scales[:],
        in_=grouped[:].rearrange("p g m t -> p (g m t)"),
    )


def rope(nc, work, results, x, coefficients, heads):
    products = work.tile([P, 2, BANK], F32)
    shape = [P, 2, heads, HEAD]
    nc.vector.tensor_tensor(
        out=products[:, :, : heads * HEAD].rearrange("p s (h d) -> p s h d", h=heads),
        in0=x.rearrange("p (h d) -> p h d", h=heads).unsqueeze(1).to_broadcast(shape),
        in1=coefficients[:].unsqueeze(2).to_broadcast(shape),
        op=MULT,
    )
    by_pair = products[:, :, : heads * HEAD].rearrange("p s (j e) -> p s j e", e=2)
    y = results.tile([P, BANK], F32)
    nc.vector.tensor_tensor(
        out=y[:, : heads * HEAD].rearrange("p (j e) -> p j e", e=2),
        in0=by_pair[:, 0],
        in1=by_pair[:, 1, :, ::-1],
        op=ADD,
    )
    return y


def store_heads(nc, out_heads, rows):
    nc.sync.dma_start(
        out=out_heads.rearrange("h p d -> p h d"),
        in_=rows.rearrange("p (h d) -> p h d", d=HEAD),
    )


def tile_multiqueryattention_pa_k_kernel(
    tc, tensor, w_qkv_words, w_qkv_scales, b_qkv, pos_emb, out_0, out_1, out_2
):
    nc = tc.nc
    x_dram = tensor[0]
    weight_words = w_qkv_words.bitcast(I32)
    scale_words = w_qkv_scales.bitcast(I32)
    q_ints = Q_COLS // 2

    with ExitStack() as ctx:
        keep = ctx.enter_context(tc.tile_pool(name="keep", bufs=1))
        group_pool = ctx.enter_context(tc.tile_pool(name="groups", bufs=GROUPS))
        stage = ctx.enter_context(tc.tile_pool(name="stage", bufs=2))
        q_weights = ctx.enter_context(tc.tile_pool(name="q_weights", bufs=6))
        work = ctx.enter_context(tc.tile_pool(name="work", bufs=2))
        results = ctx.enter_context(tc.tile_pool(name="results", bufs=Q_BANKS + 1))
        acc_pool = ctx.enter_context(tc.psum_pool(name="acc", bufs=1))
        psum = ctx.enter_context(tc.psum_pool(name="psum", bufs=3))
        ctx.enter_context(tc.manual_schedule())

        acc = [acc_pool.tile([P, BANK], F32, name="acc%d" % j) for j in range(Q_BANKS + 1)]
        planes = []
        x_codes = []
        x_scales = []
        q_chunks = []

        def load_q_weights():
            first = Q_CHUNK * len(q_chunks)
            words = q_weights.tile([P, Q_CHUNK, 2 * Q_COLS], U8, align_bytes=256)
            nc.sync.dma_start(
                out=words[:].bitcast(I32),
                in_=weight_words[first : first + Q_CHUNK, :, 0:q_ints].rearrange("g p w -> p g w"),
            )
            q_chunks.append(words)

        def make_plane(passes, cols, name):
            plane = keep.tile([P, passes, cols], U8, name=name, align_bytes=256)
            nc.vector.memset(plane[:].rearrange("p g n -> p (g n)").bitcast(I32), 0)
            return plane

        def multiply(g, j, words, plane):
            tokens = slice(TOKENS * (g % GROUP), TOKENS * (g % GROUP + 1))
            nc.tensor.matmul_mx(
                out=acc[j][:],
                lhsT=x_codes[g // GROUP][:, tokens].bitcast(FP8X4),
                lhsT_scale=x_scales[g // GROUP][:, tokens],
                rhs=words.bitcast(FP4X4),
                rhs_scale=plane,
                start=(g == 0),
                stop=(g == PASSES - 1),
            )

        def multiply_queries(chunk):
            for j in range(Q_BANKS):
                for i in range(Q_CHUNK):
                    g = Q_CHUNK * chunk + i
                    multiply(
                        g,
                        j,
                        q_chunks[chunk][:, i, 2 * BANK * j : 2 * BANK * (j + 1)],
                        planes[g // HALF][:, g % HALF, BANK * j : BANK * (j + 1)],
                    )

        x_tiles = []

        def load_tokens(group):
            x_raw = group_pool.tile([P, GROUP * K_PASS], BF16, tag="group", align_bytes=256)
            nc.sync.dma_start(
                out=x_raw[:], in_=x_dram[:, GROUP * K_PASS * group : GROUP * K_PASS * (group + 1)]
            )
            x_tiles.append(x_raw)

        load_tokens(0)
        for chunk in range(EARLY):
            load_q_weights()
        for group in range(1, GROUPS):
            load_tokens(group)

        rows = [4 * quadrant + i for i in range(4) for quadrant in (0, 2, 1, 3)]
        for first in range(0, PASSES, HALF):
            planes.append(make_plane(HALF, Q_COLS, "plane%d" % first))
        kv_plane = make_plane(PASSES, KV_COLS, "kv_plane")
        for row in rows:
            scale_row_load(nc, planes[0], scale_words, slice(0, HALF), slice(0, Q_COLS), row)
        for row in rows:
            scale_row_load(nc, planes[1], scale_words, slice(HALF, PASSES), slice(0, Q_COLS), row)
        for row in rows:
            scale_row_load(nc, kv_plane, scale_words, slice(0, PASSES), slice(Q_COLS, OUT_COLS), row)

        identity = keep.tile([P, P], F32)
        make_identity(nc, identity[:])
        bias_rows = keep.tile([P, OUT_COLS], BF16)
        nc.gpsimd.memset(bias_rows[:], 0.0)
        nc.scalar.dma_start(out=bias_rows[0:1, :], in_=b_qkv.unsqueeze(0))
        ones = keep.tile([P, P], BF16)
        nc.gpsimd.memset(ones[:], 1.0)
        pos = keep.tile([P, 2 * HEAD], BF16)
        nc.scalar.dma_start(out=pos[:], in_=pos_emb)

        for group in range(GROUPS):
            codes = keep.tile([P, GROUP * TOKENS], U32, name="x_codes%d" % group, align_bytes=64)
            scales = keep.tile([P, GROUP * TOKENS], U8, name="x_scales%d" % group, align_bytes=64)
            quantise_tokens(nc, psum, stage, identity, x_tiles[group], codes, scales)
            x_codes.append(codes)
            x_scales.append(scales)

        bias = keep.tile([P, OUT_COLS], BF16)
        for cols in range(0, OUT_COLS, BANK):
            spread = psum.tile([P, BANK], F32, tag="work")
            nc.tensor.matmul(
                out=spread[:], lhsT=ones[:], rhs=bias_rows[:, cols : cols + BANK], start=True, stop=True
            )
            nc.scalar.copy(out=bias[:, cols : cols + BANK], in_=spread[:])
        coefficients = keep.tile([P, 2, HEAD], BF16)
        nc.vector.tensor_copy(out=coefficients[:, 0, :], in_=pos[:, :HEAD])
        nc.vector.tensor_copy(
            out=coefficients[:, 1, :].rearrange("p (c e) -> p c e", e=2),
            in_=pos[:, HEAD:].rearrange("p (c e) -> p c e", e=2)[:, :, ::-1],
        )

        for chunk in range(PASSES // Q_CHUNK):
            if chunk >= EARLY:
                load_q_weights()
            multiply_queries(chunk)
        queries = []
        for j in range(Q_BANKS):
            x = work.tile([P, BANK], F32)
            nc.vector.tensor_tensor(out=x[:], in0=acc[j][:], in1=bias[:, BANK * j : BANK * (j + 1)], op=ADD)
            queries.append(rope(nc, work, results, x[:], coefficients, HEADS_PER_BANK))

        kv_acc = acc[Q_BANKS]
        for group in range(GROUPS):
            words = group_pool.tile([P, GROUP, 2 * KV_COLS], U8, tag="group", align_bytes=256)
            first = 0
            for count in (8,) if group < GROUPS - 1 else (4, 2, 1, 1):
                g = GROUP * group + first
                nc.sync.dma_start(
                    out=words[:, first : first + count, :].bitcast(I32),
                    in_=weight_words[g : g + count, :, q_ints:].rearrange("g p w -> p g w"),
                )
                for i in range(count):
                    multiply(g + i, Q_BANKS, words[:, first + i, :], kv_plane[:, g + i, :])
                first += count

        for j in range(Q_BANKS):
            store_heads(nc, out_0[0, HEADS_PER_BANK * j : HEADS_PER_BANK * (j + 1)], queries[j][:])
        k_cols = 2 * HEAD
        x = work.tile([P, BANK], F32)
        for cols in (slice(0, k_cols), slice(k_cols, KV_COLS)):
            nc.vector.tensor_tensor(
                out=x[:, cols], in0=kv_acc[:, cols], in1=bias[:, Q_COLS + cols.start : Q_COLS + cols.stop], op=ADD
            )
        store_heads(nc, out_2[0], x[:, k_cols:])
        keys = rope(nc, work, results, x[:, :k_cols], coefficients, 2)
        store_heads(nc, out_1[0], keys[:, :k_cols])
